import numpy as np
import ml_dtypes


def mxq(x, axis, fmt="e4m3"):
    dtype, down = {"e4m3": (ml_dtypes.float8_e4m3fn, 7), "e5m2": (ml_dtypes.float8_e5m2, 14)}[fmt]
    v = np.moveaxis(np.asarray(x, np.float32).astype(ml_dtypes.bfloat16).astype(np.float64), axis, -1)
    blocks = v.reshape(v.shape[:-1] + (-1, 32))
    amax = np.abs(blocks).max(-1, keepdims=True)
    byte = np.maximum(np.where(amax > 0, np.frexp(amax)[1] - 1 + 127, 0) - down, 1)
    scale = np.exp2(byte - 127.0)
    codes = (blocks / scale).astype(np.float32).astype(dtype).astype(np.float64)
    return np.moveaxis((codes * scale).reshape(v.shape), -1, axis)


WIDE = False


def mx_kscale(k):
    if not WIDE:
        return np.ones(k)
    levels = np.array([10, -10, 5, -5, 0])
    if k % 512:
        return np.exp2(np.random.permutation(np.resize(levels, k // 32))).repeat(32)
    a = np.empty((k // 512, 16))
    for p in range(k // 512):
        a[p, :8] = np.random.permutation(np.resize(levels, 8))
        for g in range(8):
            far = levels[np.abs(levels - a[p, g]) >= 10]
            a[p, g + 8] = far[np.random.randint(len(far))]
    return np.exp2(a.ravel()).repeat(32)


BF16 = ml_dtypes.bfloat16


def bf(x):
    return np.asarray(x, np.float32).astype(BF16)


def f64(x):
    return np.asarray(x).astype(np.float64)


B, N, F, C0, C1, E, G = 4, 1024, 256, 2048, 1024, 2, 4
EPS_L1 = 1e-12


def setup_inputs():
    s = mx_kscale(N)
    return {"node_feat": bf(np.random.standard_normal((B, N, F)) * 5.0 * s.mean() / s[:, None]),
            "edge_feat": bf(np.random.uniform(-0.5, 1.0, (B, E, N, N)) * s)}


def reference(node_feat, edge_feat):
    diag_mask = 1.0 - np.eye(N)
    e = f64(edge_feat) * diag_mask[None, None, :, :]
    e = e / np.maximum(np.abs(e).sum(-1, keepdims=True), EPS_L1)
    e = e
    aggr = mxq(e, 3, "e4m3") @ mxq(f64(node_feat)[:, None, :, :], 2, "e4m3")
    return aggr.transpose(0, 2, 1, 3).reshape(B, N, E * F)

@@ -1,0 +1,233 @@
+import concourse.mybir as mybir
+from concourse.masks import make_identity
+
+BF16 = mybir.dt.bfloat16
+F32 = mybir.dt.float32
+U32 = mybir.dt.uint32
+U8 = mybir.dt.uint8
+I32 = mybir.dt.int32
+FP8X4 = mybir.dt.float8_e4m3fn_x4
+ALU = mybir.AluOpType
+ACT = mybir.ActivationFunctionType
+
+P = 128
+GRAPHS = 4
+TYPES = 2
+NODES = 1024
+FEATS = 256
+EPS_L1 = 1e-12
+CLEAR_SIGNS = 0x7FFF7FFF
+
+SUM_PITCH = 8
+PACK = 4
+K_PASS = P * PACK
+PASSES = NODES // K_PASS
+PAIRS = PACK // 2
+WORDS = NODES // 2
+
+TILES_PER_GRAPH = NODES // P
+TILES = GRAPHS * TILES_PER_GRAPH
+
+FLOPS = 2 * GRAPHS * TYPES * NODES * NODES * FEATS
+
+SUM_LEAD = 2
+MASK_LEAD = SUM_LEAD + 2
+EDGE_LOAD_LEAD = MASK_LEAD + 3
+NODE_LOAD_LEAD = EDGE_LOAD_LEAD - 2
+STORE_LAG = 4
+VECTOR_SHARE = 4
+
+
+def tile_nodeupdatenetwork_pa_t_kernel(tc, node_feat, edge_feat, out):
+    nc = tc.nc
+
+    with tc.tile_pool(name="const", bufs=1) as const, tc.tile_pool(
+        name="edges", bufs=EDGE_LOAD_LEAD + 2
+    ) as edges, tc.tile_pool(name="work", bufs=3) as work, tc.tile_pool(
+        name="nodes", bufs=2
+    ) as nodes, tc.psum_pool(name="turned", bufs=4) as turned, tc.psum_pool(
+        name="sums", bufs=4
+    ) as sums:
+        identity = const.tile([P, P], F32)
+        make_identity(nc, identity[:])
+
+        table_warmer = const.tile([P, 1], F32)
+        nc.scalar.activation(out=table_warmer[:], in_=identity[:, 0:1], func=ACT.Abs)
+
+        m_of, l1_of, magnitude_of, inv_of, w_of, turned_of, grouped_of = {}, {}, {}, {}, {}, {}, {}
+        codes_of, scales_of, acc_of = {}, {}, {}
+        x_raw_of, x_grouped_of, x_codes_of, x_scales_of = {}, {}, {}, {}
+
+        def graph_and_rows(t):
+            first = (t % TILES_PER_GRAPH) * P
+            return t // TILES_PER_GRAPH, first
+
+        def load_nodes(b):
+            x_raw = nodes.tile([P, PASSES * PACK * FEATS], BF16, name="x_raw")
+            nc.sync.dma_start(
+                out=x_raw[:].rearrange("p (g r) -> p g r", r=PACK * FEATS),
+                in_=node_feat[b].rearrange("(g p t) f -> p g (t f)", p=P, t=PACK),
+            )
+            x_raw_of[b] = x_raw
+
+        def group_nodes(b):
+            x_grouped = nodes.tile([P, PASSES * FEATS * PACK], BF16, name="x_grouped", align_bytes=64)
+            src = x_raw_of[b][:].rearrange("p (g t f) -> p g t f", g=PASSES, t=PACK)
+            dst = x_grouped[:].rearrange("p (g f t) -> p g f t", g=PASSES, t=PACK)
+            for g in range(PASSES):
+                nc.vector.tensor_copy(out=dst[:, g], in_=src[:, g].rearrange("p t f -> p f t"))
+            x_grouped_of[b] = x_grouped
+
+        def quantise_nodes(b):
+            x_codes = nodes.tile([P, PASSES * FEATS], U32, name="x_codes", align_bytes=64)
+            x_scales = nodes.tile([P, PASSES * FEATS], U8, name="x_scales", align_bytes=64)
+            nc.vector.quantize_mx(out=x_codes[:].bitcast(FP8X4), scales=x_scales[:], in_=x_grouped_of[b][:])
+            x_codes_of[b], x_scales_of[b] = x_codes, x_scales
+
+        def load_edges(t):
+            b, first = graph_and_rows(t)
+            m = edges.tile([P, TYPES, NODES], BF16, name="m")
+            nc.sync.dma_start(out=m[:], in_=edge_feat[b, :, first : first + P, :].rearrange("e p k -> p e k"))
+            m_of[t] = m
+
+        def mask_self_edges(t):
+            b, first = graph_and_rows(t)
+            for e in range(TYPES):
+                block = m_of[t][:, e, first : first + P]
+                nc.gpsimd.affine_select(
+                    out=block,
+                    in_=block,
+                    pattern=[[-1, P]],
+                    compare_op=ALU.not_equal,
+                    fill=0.0,
+                    base=0,
+                    channel_multiplier=1,
+                )
+
+        def sum_type_0(t):
+            l1 = work.tile([P, TYPES, SUM_PITCH], F32, name="l1", bufs=SUM_LEAD + 3)
+            unread = work.tile([P, NODES], BF16, name="unread", bufs=4)
+            nc.scalar.activation(out=unread[:], in_=m_of[t][:, 0, :], func=ACT.Abs, accum_out=l1[:, 0, 0:1])
+            l1_of[t] = l1
+
+        def magnitude_type_1(t):
+            magnitude = work.tile([P, NODES], BF16, name="magnitude")
+            nc.vector.tensor_scalar(
+                out=magnitude[:].bitcast(I32),
+                in0=m_of[t][:, 1, :].bitcast(I32),
+                scalar1=CLEAR_SIGNS,
+                scalar2=None,
+                op0=ALU.bitwise_and,
+            )
+            magnitude_of[t] = magnitude
+
+        def sum_type_1(t):
+            unread = work.tile([P, NODES], BF16, name="unread_too")
+            nc.vector.tensor_scalar(
+                out=unread[:],
+                in0=magnitude_of[t][:],
+                scalar1=1.0,
+                scalar2=None,
+                op0=ALU.mult,
+                op1=ALU.add,
+                accum_out=l1_of[t][:, 1, 0:1],
+            )
+
+        def clamp_sums(t):
+            inv = work.tile([P, TYPES], F32, name="inv")
+            nc.vector.tensor_scalar(out=inv[:], in0=l1_of[t][:, :, 0], scalar1=EPS_L1, scalar2=None, op0=ALU.max)
+            inv_of[t] = inv
+
+        def invert_sums(t):
+            nc.vector.reciprocal(out=inv_of[t][:], in_=inv_of[t][:])
+
+        def normalise(t, e):
+            if e == 0:
+                w_of[t] = work.tile([P, TYPES * NODES], BF16, name="w")
+            nc.vector.tensor_scalar(
+                out=w_of[t][:, e * NODES : (e + 1) * NODES],
+                in0=m_of[t][:, e, :],
+                scalar1=inv_of[t][:, e : e + 1],
+                scalar2=None,
+                op0=ALU.mult,
+            )
+
+        def transpose(t):
+            words = w_of[t][:].bitcast(F32)
+            for e in range(TYPES):
+                w_t = turned.tile([P, WORDS], F32, name="w_t")
+                for q in range(WORDS // P):
+                    g, u = q // PAIRS, q % PAIRS
+                    first = e * WORDS + g * PAIRS * P
+                    every_2nd = words[:, first + u : first + PAIRS * P : PAIRS]
+                    nc.tensor.transpose(w_t[:, q * P : (q + 1) * P], every_2nd, identity[:])
+                turned_of[t, e] = w_t
+
+        def group(t, e):
+            if e == 0:
+                grouped_of[t] = work.tile([P, TYPES * PASSES * P * PACK], BF16, name="grouped", align_bytes=64)
+            dst = grouped_of[t][:].bitcast(F32).rearrange("p (e g n u) -> p e g n u", e=TYPES, g=PASSES, u=PAIRS)
+            src = turned_of[t, e][:].rearrange("p (g u n) -> p g n u", g=PASSES, u=PAIRS)
+            nc.scalar.copy(out=dst[:, e], in_=src)
+
+        def quantise(t):
+            codes = work.tile([P, TYPES * PASSES * P], U32, name="codes", align_bytes=64)
+            scales = work.tile([P, TYPES * PASSES * P], U8, name="scales", align_bytes=64)
+            nc.vector.quantize_mx(out=codes[:].bitcast(FP8X4), scales=scales[:], in_=grouped_of[t][:])
+            codes_of[t], scales_of[t] = codes, scales
+
+        def multiply(t):
+            b, first = graph_and_rows(t)
+            acc = sums.tile([P, TYPES * FEATS], F32, name="acc")
+            for e in range(TYPES):
+                for g in range(PASSES):
+                    n_cols = slice((e * PASSES + g) * P, (e * PASSES + g + 1) * P)
+                    f_cols = slice(g * FEATS, (g + 1) * FEATS)
+                    nc.tensor.matmul_mx(
+                        out=acc[:, e * FEATS : (e + 1) * FEATS],
+                        lhsT=codes_of[t][:, n_cols].bitcast(FP8X4),
+                        lhsT_scale=scales_of[t][:, n_cols],
+                        rhs=x_codes_of[b][:, f_cols].bitcast(FP8X4),
+                        rhs_scale=x_scales_of[b][:, f_cols],
+                        start=(g == 0),
+                        stop=(g == PASSES - 1),
+                    )
+            acc_of[t] = acc
+
+        def store(t):
+            b, first = graph_and_rows(t)
+            result = work.tile([P, TYPES * FEATS], F32, name="result")
+            if t % VECTOR_SHARE == VECTOR_SHARE - 1:
+                nc.vector.tensor_copy(out=result[:], in_=acc_of[t][:])
+            else:
+                nc.scalar.copy(out=result[:], in_=acc_of[t][:])
+            nc.sync.dma_start(out=out[b, first : first + P, :], in_=result[:])
+
+        def for_tile(t, stage):
+            if 0 <= t < TILES:
+                stage(t)
+
+        def for_graph_starting_at(t, stage):
+            if 0 <= t < TILES and t % TILES_PER_GRAPH == 0:
+                stage(t // TILES_PER_GRAPH)
+
+        with tc.manual_schedule():
+            for step in range(-EDGE_LOAD_LEAD, TILES + STORE_LAG + 1):
+                for_tile(step + EDGE_LOAD_LEAD, load_edges)
+                for_graph_starting_at(step + NODE_LOAD_LEAD, load_nodes)
+                for_tile(step + MASK_LEAD, mask_self_edges)
+                for_tile(step + SUM_LEAD, sum_type_0)
+                for_tile(step, magnitude_type_1)
+                for_tile(step - 1, lambda t: normalise(t, 0))
+                for_tile(step, sum_type_1)
+                for_tile(step - 1, lambda t: normalise(t, 1))
+                for_tile(step - 1, transpose)
+                for_tile(step, clamp_sums)
+                for_tile(step - 3, quantise)
+                for_tile(step - 3, multiply)
+                for_tile(step, invert_sums)
+                for_tile(step - 2, lambda t: group(t, 0))
+                for_tile(step - 2, lambda t: group(t, 1))
+                for_tile(step - STORE_LAG, store)
+                for_graph_starting_at(step - 2, quantise_nodes)
+                for_graph_starting_at(step - 1, group_nodes)

@@ -30,12 +30,15 @@ TILES = GRAPHS * TILES_PER_GRAPH
 
 FLOPS = 2 * GRAPHS * TYPES * NODES * NODES * FEATS
 
+FOLDED = 384
+FOLD_WIDTH = 64
+
 SUM_LEAD = 2
+MAGNITUDE_LEAD = 1
 MASK_LEAD = SUM_LEAD + 2
 EDGE_LOAD_LEAD = MASK_LEAD + 3
 NODE_LOAD_LEAD = EDGE_LOAD_LEAD - 2
 STORE_LAG = 4
-VECTOR_SHARE = 4
 
 
 def tile_nodeupdatenetwork_pa_t_kernel(tc, node_feat, edge_feat, out):
@@ -46,15 +49,19 @@ def tile_nodeupdatenetwork_pa_t_kernel(tc, node_feat, edge_feat, out):
     ) as edges, tc.tile_pool(name="work", bufs=3) as work, tc.tile_pool(
         name="nodes", bufs=2
     ) as nodes, tc.psum_pool(name="turned", bufs=4) as turned, tc.psum_pool(
-        name="sums", bufs=4
-    ) as sums:
+        name="sums", bufs=3
+    ) as sums, tc.psum_pool(name="folds", bufs=1) as folds:
         identity = const.tile([P, P], F32)
         make_identity(nc, identity[:])
+
+        identity_bf16 = const.tile([P, P], BF16)
+        make_identity(nc, identity_bf16[:])
 
         table_warmer = const.tile([P, 1], F32)
         nc.scalar.activation(out=table_warmer[:], in_=identity[:, 0:1], func=ACT.Abs)
 
         m_of, l1_of, magnitude_of, inv_of, w_of, turned_of, grouped_of = {}, {}, {}, {}, {}, {}, {}
+        partial_of, fold_of = {}, {}
         codes_of, scales_of, acc_of = {}, {}, {}
         x_raw_of, x_grouped_of, x_codes_of, x_scales_of = {}, {}, {}, {}
 
@@ -105,16 +112,42 @@ def tile_nodeupdatenetwork_pa_t_kernel(tc, node_feat, edge_feat, out):
                 )
 
         def sum_type_0(t):
-            l1 = work.tile([P, TYPES, SUM_PITCH], F32, name="l1", bufs=SUM_LEAD + 3)
-            unread = work.tile([P, NODES], BF16, name="unread", bufs=4)
-            nc.scalar.activation(out=unread[:], in_=m_of[t][:, 0, :], func=ACT.Abs, accum_out=l1[:, 0, 0:1])
+            partial = work.tile([P, 1], F32, name="partial", bufs=SUM_LEAD + 3)
+            unread = work.tile([P, NODES - FOLDED], BF16, name="unread", bufs=4)
+            nc.scalar.activation(
+                out=unread[:],
+                in_=m_of[t][:, 0, 0 : NODES - FOLDED],
+                func=ACT.Abs,
+                scale=1.0 / FOLD_WIDTH,
+                accum_out=partial[:],
+            )
+            partial_of[t] = partial
+
+        def fold(t):
+            fold_t = folds.tile([P, FOLD_WIDTH], F32, name="fold_t")
+            for j in range(FOLDED // FOLD_WIDTH):
+                nc.tensor.matmul(
+                    fold_t[:],
+                    lhsT=identity_bf16[:],
+                    rhs=magnitude_of[t][:, j * FOLD_WIDTH : (j + 1) * FOLD_WIDTH],
+                    start=(j == 0),
+                    stop=(j == FOLDED // FOLD_WIDTH - 1),
+                )
+            fold_of[t] = fold_t
+
+        def complete_sum_0(t):
+            l1 = work.tile([P, TYPES, SUM_PITCH], F32, name="l1")
+            unread = work.tile([P, FOLD_WIDTH], F32, name="unread_fold")
+            nc.scalar.activation(
+                out=unread[:], in_=fold_of[t][:], func=ACT.Abs, bias=partial_of[t][:], accum_out=l1[:, 0, 0:1]
+            )
             l1_of[t] = l1
 
-        def magnitude_type_1(t):
-            magnitude = work.tile([P, NODES], BF16, name="magnitude")
+        def magnitudes(t):
+            magnitude = work.tile([P, FOLDED + NODES], BF16, name="magnitude")
             nc.vector.tensor_scalar(
                 out=magnitude[:].bitcast(I32),
-                in0=m_of[t][:, 1, :].bitcast(I32),
+                in0=m_of[t][:].rearrange("p e k -> p (e k)")[:, NODES - FOLDED :].bitcast(I32),
                 scalar1=CLEAR_SIGNS,
                 scalar2=None,
                 op0=ALU.bitwise_and,
@@ -125,7 +158,7 @@ def tile_nodeupdatenetwork_pa_t_kernel(tc, node_feat, edge_feat, out):
             unread = work.tile([P, NODES], BF16, name="unread_too")
             nc.vector.tensor_scalar(
                 out=unread[:],
-                in0=magnitude_of[t][:],
+                in0=magnitude_of[t][:, FOLDED:],
                 scalar1=1.0,
                 scalar2=None,
                 op0=ALU.mult,
@@ -197,10 +230,7 @@ def tile_nodeupdatenetwork_pa_t_kernel(tc, node_feat, edge_feat, out):
         def store(t):
             b, first = graph_and_rows(t)
             result = work.tile([P, TYPES * FEATS], F32, name="result")
-            if t % VECTOR_SHARE == VECTOR_SHARE - 1:
-                nc.vector.tensor_copy(out=result[:], in_=acc_of[t][:])
-            else:
-                nc.scalar.copy(out=result[:], in_=acc_of[t][:])
+            nc.scalar.copy(out=result[:], in_=acc_of[t][:])
             nc.sync.dma_start(out=out[b, first : first + P, :], in_=result[:])
 
         def for_tile(t, stage):
@@ -217,7 +247,8 @@ def tile_nodeupdatenetwork_pa_t_kernel(tc, node_feat, edge_feat, out):
                 for_graph_starting_at(step + NODE_LOAD_LEAD, load_nodes)
                 for_tile(step + MASK_LEAD, mask_self_edges)
                 for_tile(step + SUM_LEAD, sum_type_0)
-                for_tile(step, magnitude_type_1)
+                for_tile(step + MAGNITUDE_LEAD, magnitudes)
+                for_tile(step + MAGNITUDE_LEAD, fold)
                 for_tile(step - 1, lambda t: normalise(t, 0))
                 for_tile(step, sum_type_1)
                 for_tile(step - 1, lambda t: normalise(t, 1))
@@ -228,6 +259,7 @@ def tile_nodeupdatenetwork_pa_t_kernel(tc, node_feat, edge_feat, out):
                 for_tile(step, invert_sums)
                 for_tile(step - 2, lambda t: group(t, 0))
                 for_tile(step - 2, lambda t: group(t, 1))
+                for_tile(step + MAGNITUDE_LEAD, complete_sum_0)
                 for_tile(step - STORE_LAG, store)
                 for_graph_starting_at(step - 2, quantise_nodes)
                 for_graph_starting_at(step - 1, group_nodes)

@@ -33,19 +33,21 @@ FLOPS = 2 * GRAPHS * TYPES * NODES * NODES * FEATS
 FOLDED = 384
 FOLD_WIDTH = 64
 
-SUM_LEAD = 2
-MAGNITUDE_LEAD = 1
+PAIR = 2
+SUM_1_LEAD = 2
+MAGNITUDE_LEAD = SUM_1_LEAD + 1
+SUM_LEAD = MAGNITUDE_LEAD + 1
 MASK_LEAD = SUM_LEAD + 2
 EDGE_LOAD_LEAD = MASK_LEAD + 3
-NODE_LOAD_LEAD = EDGE_LOAD_LEAD - 2
-STORE_LAG = 4
+NODE_LOAD_LEAD = EDGE_LOAD_LEAD - 4
+STORE_LAG = 3
 
 
 def tile_nodeupdatenetwork_pa_t_kernel(tc, node_feat, edge_feat, out):
     nc = tc.nc
 
     with tc.tile_pool(name="const", bufs=1) as const, tc.tile_pool(
-        name="edges", bufs=EDGE_LOAD_LEAD + 2
+        name="edges", bufs=EDGE_LOAD_LEAD + 1
     ) as edges, tc.tile_pool(name="work", bufs=3) as work, tc.tile_pool(
         name="nodes", bufs=2
     ) as nodes, tc.psum_pool(name="turned", bufs=4) as turned, tc.psum_pool(
@@ -94,7 +96,11 @@ def tile_nodeupdatenetwork_pa_t_kernel(tc, node_feat, edge_feat, out):
         def load_edges(t):
             b, first = graph_and_rows(t)
             m = edges.tile([P, TYPES, NODES], BF16, name="m")
-            nc.sync.dma_start(out=m[:], in_=edge_feat[b, :, first : first + P, :].rearrange("e p k -> p e k"))
+            if t == 0:
+                for e in range(TYPES):
+                    nc.sync.dma_start(out=m[:, e, :], in_=edge_feat[b, e, first : first + P, :])
+            else:
+                nc.sync.dma_start(out=m[:], in_=edge_feat[b, :, first : first + P, :].rearrange("e p k -> p e k"))
             m_of[t] = m
 
         def mask_self_edges(t):
@@ -112,7 +118,7 @@ def tile_nodeupdatenetwork_pa_t_kernel(tc, node_feat, edge_feat, out):
                 )
 
         def sum_type_0(t):
-            partial = work.tile([P, 1], F32, name="partial", bufs=SUM_LEAD + 3)
+            partial = work.tile([P, 1], F32, name="partial", bufs=4)
             unread = work.tile([P, NODES - FOLDED], BF16, name="unread", bufs=4)
             nc.scalar.activation(
                 out=unread[:],
@@ -136,12 +142,16 @@ def tile_nodeupdatenetwork_pa_t_kernel(tc, node_feat, edge_feat, out):
             fold_of[t] = fold_t
 
         def complete_sum_0(t):
-            l1 = work.tile([P, TYPES, SUM_PITCH], F32, name="l1")
+            if t % PAIR == 0:
+                l1_of[t // PAIR] = work.tile([P, PAIR, TYPES, SUM_PITCH], F32, name="l1")
             unread = work.tile([P, FOLD_WIDTH], F32, name="unread_fold")
             nc.scalar.activation(
-                out=unread[:], in_=fold_of[t][:], func=ACT.Abs, bias=partial_of[t][:], accum_out=l1[:, 0, 0:1]
+                out=unread[:],
+                in_=fold_of[t][:],
+                func=ACT.Abs,
+                bias=partial_of[t][:],
+                accum_out=l1_of[t // PAIR][:, t % PAIR, 0, 0:1],
             )
-            l1_of[t] = l1
 
         def magnitudes(t):
             magnitude = work.tile([P, FOLDED + NODES], BF16, name="magnitude")
@@ -163,16 +173,16 @@ def tile_nodeupdatenetwork_pa_t_kernel(tc, node_feat, edge_feat, out):
                 scalar2=None,
                 op0=ALU.mult,
                 op1=ALU.add,
-                accum_out=l1_of[t][:, 1, 0:1],
+                accum_out=l1_of[t // PAIR][:, t % PAIR, 1, 0:1],
             )
 
-        def clamp_sums(t):
-            inv = work.tile([P, TYPES], F32, name="inv")
-            nc.vector.tensor_scalar(out=inv[:], in0=l1_of[t][:, :, 0], scalar1=EPS_L1, scalar2=None, op0=ALU.max)
-            inv_of[t] = inv
+        def clamp_sums(i):
+            inv = work.tile([P, PAIR, TYPES], F32, name="inv")
+            nc.vector.tensor_scalar(out=inv[:], in0=l1_of[i][:, :, :, 0], scalar1=EPS_L1, scalar2=None, op0=ALU.max)
+            inv_of[i] = inv
 
-        def invert_sums(t):
-            nc.vector.reciprocal(out=inv_of[t][:], in_=inv_of[t][:])
+        def invert_sums(i):
+            nc.vector.reciprocal(out=inv_of[i][:], in_=inv_of[i][:])
 
         def normalise(t, e):
             if e == 0:
@@ -180,7 +190,7 @@ def tile_nodeupdatenetwork_pa_t_kernel(tc, node_feat, edge_feat, out):
             nc.vector.tensor_scalar(
                 out=w_of[t][:, e * NODES : (e + 1) * NODES],
                 in0=m_of[t][:, e, :],
-                scalar1=inv_of[t][:, e : e + 1],
+                scalar1=inv_of[t // PAIR][:, t % PAIR, e : e + 1],
                 scalar2=None,
                 op0=ALU.mult,
             )
@@ -203,35 +213,50 @@ def tile_nodeupdatenetwork_pa_t_kernel(tc, node_feat, edge_feat, out):
             src = turned_of[t, e][:].rearrange("p (g u n) -> p g n u", g=PASSES, u=PAIRS)
             nc.scalar.copy(out=dst[:, e], in_=src)
 
+        def types_together(t):
+            return [(0,), (1,)] if t == TILES - 1 else [(0, 1)]
+
         def quantise(t):
             codes = work.tile([P, TYPES * PASSES * P], U32, name="codes", align_bytes=64)
             scales = work.tile([P, TYPES * PASSES * P], U8, name="scales", align_bytes=64)
-            nc.vector.quantize_mx(out=codes[:].bitcast(FP8X4), scales=scales[:], in_=grouped_of[t][:])
+            for types in types_together(t):
+                words = slice(types[0] * PASSES * P, (types[-1] + 1) * PASSES * P)
+                nc.vector.quantize_mx(
+                    out=codes[:, words].bitcast(FP8X4),
+                    scales=scales[:, words],
+                    in_=grouped_of[t][:, words.start * PACK : words.stop * PACK],
+                )
             codes_of[t], scales_of[t] = codes, scales
 
         def multiply(t):
             b, first = graph_and_rows(t)
-            acc = sums.tile([P, TYPES * FEATS], F32, name="acc")
-            for e in range(TYPES):
-                for g in range(PASSES):
-                    n_cols = slice((e * PASSES + g) * P, (e * PASSES + g + 1) * P)
-                    f_cols = slice(g * FEATS, (g + 1) * FEATS)
-                    nc.tensor.matmul_mx(
-                        out=acc[:, e * FEATS : (e + 1) * FEATS],
-                        lhsT=codes_of[t][:, n_cols].bitcast(FP8X4),
-                        lhsT_scale=scales_of[t][:, n_cols],
-                        rhs=x_codes_of[b][:, f_cols].bitcast(FP8X4),
-                        rhs_scale=x_scales_of[b][:, f_cols],
-                        start=(g == 0),
-                        stop=(g == PASSES - 1),
-                    )
-            acc_of[t] = acc
+            for types in types_together(t):
+                acc = sums.tile([P, TYPES * FEATS], F32, name="acc")
+                for e in types:
+                    for g in range(PASSES):
+                        n_cols = slice((e * PASSES + g) * P, (e * PASSES + g + 1) * P)
+                        f_cols = slice(g * FEATS, (g + 1) * FEATS)
+                        nc.tensor.matmul_mx(
+                            out=acc[:, e * FEATS : (e + 1) * FEATS],
+                            lhsT=codes_of[t][:, n_cols].bitcast(FP8X4),
+                            lhsT_scale=scales_of[t][:, n_cols],
+                            rhs=x_codes_of[b][:, f_cols].bitcast(FP8X4),
+                            rhs_scale=x_scales_of[b][:, f_cols],
+                            start=(g == 0),
+                            stop=(g == PASSES - 1),
+                        )
+                acc_of[t, types] = acc
 
         def store(t):
             b, first = graph_and_rows(t)
-            result = work.tile([P, TYPES * FEATS], F32, name="result")
-            nc.scalar.copy(out=result[:], in_=acc_of[t][:])
-            nc.sync.dma_start(out=out[b, first : first + P, :], in_=result[:])
+            result = work.tile([P, TYPES * FEATS], F32, name="result", bufs=6)
+            for types in types_together(t):
+                columns = slice(types[0] * FEATS, (types[-1] + 1) * FEATS)
+                if t in (TILES - 4, TILES - 2) or types == (1,):
+                    nc.vector.tensor_copy(out=result[:, columns], in_=acc_of[t, types][:, columns])
+                else:
+                    nc.scalar.copy(out=result[:, columns], in_=acc_of[t, types][:, columns])
+                nc.sync.dma_start(out=out[b, first : first + P, columns], in_=result[:, columns])
 
         def for_tile(t, stage):
             if 0 <= t < TILES:
@@ -241,25 +266,29 @@ def tile_nodeupdatenetwork_pa_t_kernel(tc, node_feat, edge_feat, out):
             if 0 <= t < TILES and t % TILES_PER_GRAPH == 0:
                 stage(t // TILES_PER_GRAPH)
 
+        def for_pair_starting_at(t, stage):
+            if 0 <= t < TILES and t % PAIR == 0:
+                stage(t // PAIR)
+
         with tc.manual_schedule():
-            for step in range(-EDGE_LOAD_LEAD, TILES + STORE_LAG + 1):
+            for step in range(-EDGE_LOAD_LEAD, TILES + STORE_LAG):
                 for_tile(step + EDGE_LOAD_LEAD, load_edges)
                 for_graph_starting_at(step + NODE_LOAD_LEAD, load_nodes)
                 for_tile(step + MASK_LEAD, mask_self_edges)
                 for_tile(step + SUM_LEAD, sum_type_0)
                 for_tile(step + MAGNITUDE_LEAD, magnitudes)
                 for_tile(step + MAGNITUDE_LEAD, fold)
-                for_tile(step - 1, lambda t: normalise(t, 0))
-                for_tile(step, sum_type_1)
-                for_tile(step - 1, lambda t: normalise(t, 1))
-                for_tile(step - 1, transpose)
-                for_tile(step, clamp_sums)
-                for_tile(step - 3, quantise)
-                for_tile(step - 3, multiply)
-                for_tile(step, invert_sums)
-                for_tile(step - 2, lambda t: group(t, 0))
-                for_tile(step - 2, lambda t: group(t, 1))
+                for_tile(step, lambda t: normalise(t, 0))
+                for_tile(step + SUM_1_LEAD, sum_type_1)
+                for_tile(step, lambda t: normalise(t, 1))
+                for_tile(step, transpose)
+                for_pair_starting_at(step + 1, clamp_sums)
+                for_tile(step - 2, quantise)
+                for_tile(step - 2, multiply)
+                for_pair_starting_at(step + 1, invert_sums)
+                for_tile(step - 1, lambda t: group(t, 0))
+                for_tile(step - 1, lambda t: group(t, 1))
                 for_tile(step + MAGNITUDE_LEAD, complete_sum_0)
                 for_tile(step - STORE_LAG, store)
-                for_graph_starting_at(step - 2, quantise_nodes)
-                for_graph_starting_at(step - 1, group_nodes)
+                for_graph_starting_at(step - 1, quantise_nodes)
+                for_graph_starting_at(step, group_nodes)

@@ -23,6 +23,7 @@ PACK = 4
 K_PASS = P * PACK
 PASSES = NODES // K_PASS
 PAIRS = PACK // 2
+RUN = 4
 WORDS = NODES // 2
 
 TILES_PER_GRAPH = NODES // P
@@ -73,10 +74,16 @@ def tile_nodeupdatenetwork_pa_t_kernel(tc, node_feat, edge_feat, out):
 
         def load_nodes(b):
             x_raw = nodes.tile([P, PASSES * PACK * FEATS], BF16, name="x_raw")
-            nc.sync.dma_start(
-                out=x_raw[:].rearrange("p (g r) -> p g r", r=PACK * FEATS),
-                in_=node_feat[b].rearrange("(g p t) f -> p g (t f)", p=P, t=PACK),
-            )
+            for g in range(PASSES):
+                rows = node_feat[b, g * K_PASS : (g + 1) * K_PASS, :]
+                rows = rows.rearrange("(j u i h) f -> i j u (h f)", u=PAIRS, i=RUN, h=2)
+                for i in range(RUN):
+                    nc.sync.dma_start(
+                        out=x_raw[i::RUN, g * PACK * FEATS : (g + 1) * PACK * FEATS].rearrange(
+                            "p (u r) -> p u r", u=PAIRS
+                        ),
+                        in_=rows[i],
+                    )
             x_raw_of[b] = x_raw
 
         def group_nodes(b):
@@ -188,8 +195,8 @@ def tile_nodeupdatenetwork_pa_t_kernel(tc, node_feat, edge_feat, out):
             if e == 0:
                 w_of[t] = work.tile([P, TYPES * NODES], BF16, name="w")
             nc.vector.tensor_scalar(
-                out=w_of[t][:, e * NODES : (e + 1) * NODES],
-                in0=m_of[t][:, e, :],
+                out=w_of[t][:, e * NODES : (e + 1) * NODES].rearrange("p (u j r) -> p u j r", u=PAIRS, r=2 * RUN),
+                in0=m_of[t][:, e, :].rearrange("p (j u r) -> p u j r", u=PAIRS, r=2 * RUN),
                 scalar1=inv_of[t // PAIR][:, t % PAIR, e : e + 1],
                 scalar2=None,
                 op0=ALU.mult,
@@ -201,9 +208,8 @@ def tile_nodeupdatenetwork_pa_t_kernel(tc, node_feat, edge_feat, out):
                 w_t = turned.tile([P, WORDS], F32, name="w_t")
                 for q in range(WORDS // P):
                     g, u = q // PAIRS, q % PAIRS
-                    first = e * WORDS + g * PAIRS * P
-                    every_2nd = words[:, first + u : first + PAIRS * P : PAIRS]
-                    nc.tensor.transpose(w_t[:, q * P : (q + 1) * P], every_2nd, identity[:])
+                    first = e * WORDS + (u * PASSES + g) * P
+                    nc.tensor.transpose(w_t[:, q * P : (q + 1) * P], words[:, first : first + P], identity[:])
                 turned_of[t, e] = w_t
 
         def group(t, e):

@@ -31,8 +31,9 @@ TILES = GRAPHS * TILES_PER_GRAPH
 
 FLOPS = 2 * GRAPHS * TYPES * NODES * NODES * FEATS
 
-FOLDED = 384
-FOLD_WIDTH = 64
+FOLDED = 400
+FOLD_1_EVERY = 8
+FOLD_WIDTH = 50
 
 PAIR = 2
 SUM_1_LEAD = 2
@@ -124,17 +125,22 @@ def tile_nodeupdatenetwork_pa_t_kernel(tc, node_feat, edge_feat, out):
                     channel_multiplier=1,
                 )
 
+        def folded_type(t):
+            return 1 if t % FOLD_1_EVERY == FOLD_1_EVERY - 1 else 0
+
         def sum_type_0(t):
-            partial = work.tile([P, 1], F32, name="partial", bufs=4)
-            unread = work.tile([P, NODES - FOLDED], BF16, name="unread", bufs=4)
+            if t % PAIR == 0:
+                l1_of[t // PAIR] = work.tile([P, PAIR, TYPES, SUM_PITCH], F32, name="l1", bufs=4)
+            partial_of[t] = work.tile([P, 1], F32, name="partial", bufs=4)
+            unread = work.tile([P, NODES], BF16, name="unread", bufs=4)
+            columns = NODES - FOLDED if folded_type(t) == 0 else NODES
             nc.scalar.activation(
-                out=unread[:],
-                in_=m_of[t][:, 0, 0 : NODES - FOLDED],
+                out=unread[:, 0:columns],
+                in_=m_of[t][:, 0, 0:columns],
                 func=ACT.Abs,
-                scale=1.0 / FOLD_WIDTH,
-                accum_out=partial[:],
+                scale=1.0 / FOLD_WIDTH if folded_type(t) == 0 else 1.0,
+                accum_out=partial_of[t][:] if folded_type(t) == 0 else l1_of[t // PAIR][:, t % PAIR, 0, 0:1],
             )
-            partial_of[t] = partial
 
         def fold(t):
             fold_t = folds.tile([P, FOLD_WIDTH], F32, name="fold_t")
@@ -148,36 +154,40 @@ def tile_nodeupdatenetwork_pa_t_kernel(tc, node_feat, edge_feat, out):
                 )
             fold_of[t] = fold_t
 
-        def complete_sum_0(t):
-            if t % PAIR == 0:
-                l1_of[t // PAIR] = work.tile([P, PAIR, TYPES, SUM_PITCH], F32, name="l1")
+        def sum_fold(t):
             unread = work.tile([P, FOLD_WIDTH], F32, name="unread_fold")
-            nc.scalar.activation(
-                out=unread[:],
-                in_=fold_of[t][:],
-                func=ACT.Abs,
-                bias=partial_of[t][:],
-                accum_out=l1_of[t // PAIR][:, t % PAIR, 0, 0:1],
-            )
+            if folded_type(t) == 0:
+                nc.scalar.activation(
+                    out=unread[:],
+                    in_=fold_of[t][:],
+                    func=ACT.Abs,
+                    bias=partial_of[t][:],
+                    accum_out=l1_of[t // PAIR][:, t % PAIR, 0, 0:1],
+                )
+            else:
+                nc.scalar.activation(out=unread[:], in_=fold_of[t][:], func=ACT.Abs, accum_out=partial_of[t][:])
 
         def magnitudes(t):
+            first = NODES - FOLDED if folded_type(t) == 0 else NODES
+            width = TYPES * NODES - first
             magnitude = work.tile([P, FOLDED + NODES], BF16, name="magnitude")
             nc.vector.tensor_scalar(
-                out=magnitude[:].bitcast(I32),
-                in0=m_of[t][:].rearrange("p e k -> p (e k)")[:, NODES - FOLDED :].bitcast(I32),
+                out=magnitude[:, 0:width].bitcast(I32),
+                in0=m_of[t][:].rearrange("p e k -> p (e k)")[:, first:].bitcast(I32),
                 scalar1=CLEAR_SIGNS,
                 scalar2=None,
                 op0=ALU.bitwise_and,
             )
-            magnitude_of[t] = magnitude
+            magnitude_of[t] = magnitude[:, 0:width]
 
         def sum_type_1(t):
+            magnitude = magnitude_of[t][:, FOLDED:]
             unread = work.tile([P, NODES], BF16, name="unread_too")
             nc.vector.tensor_scalar(
-                out=unread[:],
-                in0=magnitude_of[t][:, FOLDED:],
+                out=unread[:, 0 : magnitude.shape[1]],
+                in0=magnitude,
                 scalar1=1.0,
-                scalar2=None,
+                scalar2=partial_of[t][:] if folded_type(t) == 1 else None,
                 op0=ALU.mult,
                 op1=ALU.add,
                 accum_out=l1_of[t // PAIR][:, t % PAIR, 1, 0:1],
@@ -294,7 +304,7 @@ def tile_nodeupdatenetwork_pa_t_kernel(tc, node_feat, edge_feat, out):
                 for_pair_starting_at(step + 1, invert_sums)
                 for_tile(step - 1, lambda t: group(t, 0))
                 for_tile(step - 1, lambda t: group(t, 1))
-                for_tile(step + MAGNITUDE_LEAD, complete_sum_0)
+                for_tile(step + MAGNITUDE_LEAD, sum_fold)
                 for_tile(step - STORE_LAG, store)
                 for_graph_starting_at(step - 1, quantise_nodes)
                 for_graph_starting_at(step, group_nodes)

import concourse.mybir as mybir
from concourse.masks import make_identity

BF16 = mybir.dt.bfloat16
F32 = mybir.dt.float32
U32 = mybir.dt.uint32
U8 = mybir.dt.uint8
I32 = mybir.dt.int32
FP8X4 = mybir.dt.float8_e4m3fn_x4
ALU = mybir.AluOpType
ACT = mybir.ActivationFunctionType

P = 128
GRAPHS = 4
TYPES = 2
NODES = 1024
FEATS = 256
EPS_L1 = 1e-12
CLEAR_SIGNS = 0x7FFF7FFF

SUM_PITCH = 8
PACK = 4
K_PASS = P * PACK
PASSES = NODES // K_PASS
PAIRS = PACK // 2
RUN = 4
WORDS = NODES // 2

TILES_PER_GRAPH = NODES // P
TILES = GRAPHS * TILES_PER_GRAPH

FLOPS = 2 * GRAPHS * TYPES * NODES * NODES * FEATS

FOLDED = 400
FOLD_1_EVERY = 8
FOLD_WIDTH = 50

PAIR = 2
SUM_1_LEAD = 2
MAGNITUDE_LEAD = SUM_1_LEAD + 1
SUM_LEAD = MAGNITUDE_LEAD + 1
MASK_LEAD = SUM_LEAD + 2
EDGE_LOAD_LEAD = MASK_LEAD + 3
NODE_LOAD_LEAD = EDGE_LOAD_LEAD - 4
STORE_LAG = 3


def tile_nodeupdatenetwork_pa_t_kernel(tc, node_feat, edge_feat, out):
    nc = tc.nc

    with tc.tile_pool(name="const", bufs=1) as const, tc.tile_pool(
        name="edges", bufs=EDGE_LOAD_LEAD + 1
    ) as edges, tc.tile_pool(name="work", bufs=3) as work, tc.tile_pool(
        name="nodes", bufs=2
    ) as nodes, tc.psum_pool(name="turned", bufs=4) as turned, tc.psum_pool(
        name="sums", bufs=3
    ) as sums, tc.psum_pool(name="folds", bufs=1) as folds:
        identity = const.tile([P, P], F32)
        make_identity(nc, identity[:])

        identity_bf16 = const.tile([P, P], BF16)
        make_identity(nc, identity_bf16[:])

        table_warmer = const.tile([P, 1], F32)
        nc.scalar.activation(out=table_warmer[:], in_=identity[:, 0:1], func=ACT.Abs)

        m_of, l1_of, magnitude_of, inv_of, w_of, turned_of, grouped_of = {}, {}, {}, {}, {}, {}, {}
        partial_of, fold_of = {}, {}
        codes_of, scales_of, acc_of = {}, {}, {}
        x_raw_of, x_grouped_of, x_codes_of, x_scales_of = {}, {}, {}, {}

        def graph_and_rows(t):
            first = (t % TILES_PER_GRAPH) * P
            return t // TILES_PER_GRAPH, first

        def load_nodes(b):
            x_raw = nodes.tile([P, PASSES * PACK * FEATS], BF16, name="x_raw")
            for g in range(PASSES):
                rows = node_feat[b, g * K_PASS : (g + 1) * K_PASS, :]
                rows = rows.rearrange("(j u i h) f -> i j u (h f)", u=PAIRS, i=RUN, h=2)
                for i in range(RUN):
                    nc.sync.dma_start(
                        out=x_raw[i::RUN, g * PACK * FEATS : (g + 1) * PACK * FEATS].rearrange(
                            "p (u r) -> p u r", u=PAIRS
                        ),
                        in_=rows[i],
                    )
            x_raw_of[b] = x_raw

        def group_nodes(b):
            x_grouped = nodes.tile([P, PASSES * FEATS * PACK], BF16, name="x_grouped", align_bytes=64)
            src = x_raw_of[b][:].rearrange("p (g t f) -> p g t f", g=PASSES, t=PACK)
            dst = x_grouped[:].rearrange("p (g f t) -> p g f t", g=PASSES, t=PACK)
            for g in range(PASSES):
                nc.vector.tensor_copy(out=dst[:, g], in_=src[:, g].rearrange("p t f -> p f t"))
            x_grouped_of[b] = x_grouped

        def quantise_nodes(b):
            x_codes = nodes.tile([P, PASSES * FEATS], U32, name="x_codes", align_bytes=64)
            x_scales = nodes.tile([P, PASSES * FEATS], U8, name="x_scales", align_bytes=64)
            nc.vector.quantize_mx(out=x_codes[:].bitcast(FP8X4), scales=x_scales[:], in_=x_grouped_of[b][:])
            x_codes_of[b], x_scales_of[b] = x_codes, x_scales

        def load_edges(t):
            b, first = graph_and_rows(t)
            m = edges.tile([P, TYPES, NODES], BF16, name="m")
            if t == 0:
                for e in range(TYPES):
                    nc.sync.dma_start(out=m[:, e, :], in_=edge_feat[b, e, first : first + P, :])
            else:
                nc.sync.dma_start(out=m[:], in_=edge_feat[b, :, first : first + P, :].rearrange("e p k -> p e k"))
            m_of[t] = m

        def mask_self_edges(t):
            b, first = graph_and_rows(t)
            for e in range(TYPES):
                block = m_of[t][:, e, first : first + P]
                nc.gpsimd.affine_select(
                    out=block,
                    in_=block,
                    pattern=[[-1, P]],
                    compare_op=ALU.not_equal,
                    fill=0.0,
                    base=0,
                    channel_multiplier=1,
                )

        def folded_type(t):
            return 1 if t % FOLD_1_EVERY == FOLD_1_EVERY - 1 else 0

        def sum_type_0(t):
            if t % PAIR == 0:
                l1_of[t // PAIR] = work.tile([P, PAIR, TYPES, SUM_PITCH], F32, name="l1", bufs=4)
            partial_of[t] = work.tile([P, 1], F32, name="partial", bufs=4)
            unread = work.tile([P, NODES], BF16, name="unread", bufs=4)
            columns = NODES - FOLDED if folded_type(t) == 0 else NODES
            nc.scalar.activation(
                out=unread[:, 0:columns],
                in_=m_of[t][:, 0, 0:columns],
                func=ACT.Abs,
                scale=1.0 / FOLD_WIDTH if folded_type(t) == 0 else 1.0,
                accum_out=partial_of[t][:] if folded_type(t) == 0 else l1_of[t // PAIR][:, t % PAIR, 0, 0:1],
            )

        def fold(t):
            fold_t = folds.tile([P, FOLD_WIDTH], F32, name="fold_t")
            for j in range(FOLDED // FOLD_WIDTH):
                nc.tensor.matmul(
                    fold_t[:],
                    lhsT=identity_bf16[:],
                    rhs=magnitude_of[t][:, j * FOLD_WIDTH : (j + 1) * FOLD_WIDTH],
                    start=(j == 0),
                    stop=(j == FOLDED // FOLD_WIDTH - 1),
                )
            fold_of[t] = fold_t

        def sum_fold(t):
            unread = work.tile([P, FOLD_WIDTH], F32, name="unread_fold")
            if folded_type(t) == 0:
                nc.scalar.activation(
                    out=unread[:],
                    in_=fold_of[t][:],
                    func=ACT.Abs,
                    bias=partial_of[t][:],
                    accum_out=l1_of[t // PAIR][:, t % PAIR, 0, 0:1],
                )
            else:
                nc.scalar.activation(out=unread[:], in_=fold_of[t][:], func=ACT.Abs, accum_out=partial_of[t][:])

        def magnitudes(t):
            first = NODES - FOLDED if folded_type(t) == 0 else NODES
            width = TYPES * NODES - first
            magnitude = work.tile([P, FOLDED + NODES], BF16, name="magnitude")
            nc.vector.tensor_scalar(
                out=magnitude[:, 0:width].bitcast(I32),
                in0=m_of[t][:].rearrange("p e k -> p (e k)")[:, first:].bitcast(I32),
                scalar1=CLEAR_SIGNS,
                scalar2=None,
                op0=ALU.bitwise_and,
            )
            magnitude_of[t] = magnitude[:, 0:width]

        def sum_type_1(t):
            magnitude = magnitude_of[t][:, FOLDED:]
            unread = work.tile([P, NODES], BF16, name="unread_too")
            nc.vector.tensor_scalar(
                out=unread[:, 0 : magnitude.shape[1]],
                in0=magnitude,
                scalar1=1.0,
                scalar2=partial_of[t][:] if folded_type(t) == 1 else None,
                op0=ALU.mult,
                op1=ALU.add,
                accum_out=l1_of[t // PAIR][:, t % PAIR, 1, 0:1],
            )

        def clamp_sums(i):
            inv = work.tile([P, PAIR, TYPES], F32, name="inv")
            nc.vector.tensor_scalar(out=inv[:], in0=l1_of[i][:, :, :, 0], scalar1=EPS_L1, scalar2=None, op0=ALU.max)
            inv_of[i] = inv

        def invert_sums(i):
            nc.vector.reciprocal(out=inv_of[i][:], in_=inv_of[i][:])

        def normalise(t, e):
            if e == 0:
                w_of[t] = work.tile([P, TYPES * NODES], BF16, name="w")
            nc.vector.tensor_scalar(
                out=w_of[t][:, e * NODES : (e + 1) * NODES].rearrange("p (u j r) -> p u j r", u=PAIRS, r=2 * RUN),
                in0=m_of[t][:, e, :].rearrange("p (j u r) -> p u j r", u=PAIRS, r=2 * RUN),
                scalar1=inv_of[t // PAIR][:, t % PAIR, e : e + 1],
                scalar2=None,
                op0=ALU.mult,
            )

        def transpose(t):
            words = w_of[t][:].bitcast(F32)
            for e in range(TYPES):
                w_t = turned.tile([P, WORDS], F32, name="w_t")
                for q in range(WORDS // P):
                    g, u = q // PAIRS, q % PAIRS
                    first = e * WORDS + (u * PASSES + g) * P
                    nc.tensor.transpose(w_t[:, q * P : (q + 1) * P], words[:, first : first + P], identity[:])
                turned_of[t, e] = w_t

        def group(t, e):
            if e == 0:
                grouped_of[t] = work.tile([P, TYPES * PASSES * P * PACK], BF16, name="grouped", align_bytes=64)
            dst = grouped_of[t][:].bitcast(F32).rearrange("p (e g n u) -> p e g n u", e=TYPES, g=PASSES, u=PAIRS)
            src = turned_of[t, e][:].rearrange("p (g u n) -> p g n u", g=PASSES, u=PAIRS)
            nc.scalar.copy(out=dst[:, e], in_=src)

        def types_together(t):
            return [(0,), (1,)] if t == TILES - 1 else [(0, 1)]

        def quantise(t):
            codes = work.tile([P, TYPES * PASSES * P], U32, name="codes", align_bytes=64)
            scales = work.tile([P, TYPES * PASSES * P], U8, name="scales", align_bytes=64)
            for types in types_together(t):
                words = slice(types[0] * PASSES * P, (types[-1] + 1) * PASSES * P)
                nc.vector.quantize_mx(
                    out=codes[:, words].bitcast(FP8X4),
                    scales=scales[:, words],
                    in_=grouped_of[t][:, words.start * PACK : words.stop * PACK],
                )
            codes_of[t], scales_of[t] = codes, scales

        def multiply(t):
            b, first = graph_and_rows(t)
            for types in types_together(t):
                acc = sums.tile([P, TYPES * FEATS], F32, name="acc")
                for e in types:
                    for g in range(PASSES):
                        n_cols = slice((e * PASSES + g) * P, (e * PASSES + g + 1) * P)
                        f_cols = slice(g * FEATS, (g + 1) * FEATS)
                        nc.tensor.matmul_mx(
                            out=acc[:, e * FEATS : (e + 1) * FEATS],
                            lhsT=codes_of[t][:, n_cols].bitcast(FP8X4),
                            lhsT_scale=scales_of[t][:, n_cols],
                            rhs=x_codes_of[b][:, f_cols].bitcast(FP8X4),
                            rhs_scale=x_scales_of[b][:, f_cols],
                            start=(g == 0),
                            stop=(g == PASSES - 1),
                        )
                acc_of[t, types] = acc

        def store(t):
            b, first = graph_and_rows(t)
            result = work.tile([P, TYPES * FEATS], F32, name="result", bufs=6)
            for types in types_together(t):
                columns = slice(types[0] * FEATS, (types[-1] + 1) * FEATS)
                if t in (TILES - 4, TILES - 2) or types == (1,):
                    nc.vector.tensor_copy(out=result[:, columns], in_=acc_of[t, types][:, columns])
                else:
                    nc.scalar.copy(out=result[:, columns], in_=acc_of[t, types][:, columns])
                nc.sync.dma_start(out=out[b, first : first + P, columns], in_=result[:, columns])

        def for_tile(t, stage):
            if 0 <= t < TILES:
                stage(t)

        def for_graph_starting_at(t, stage):
            if 0 <= t < TILES and t % TILES_PER_GRAPH == 0:
                stage(t // TILES_PER_GRAPH)

        def for_pair_starting_at(t, stage):
            if 0 <= t < TILES and t % PAIR == 0:
                stage(t // PAIR)

        with tc.manual_schedule():
            for step in range(-EDGE_LOAD_LEAD, TILES + STORE_LAG):
                for_tile(step + EDGE_LOAD_LEAD, load_edges)
                for_graph_starting_at(step + NODE_LOAD_LEAD, load_nodes)
                for_tile(step + MASK_LEAD, mask_self_edges)
                for_tile(step + SUM_LEAD, sum_type_0)
                for_tile(step + MAGNITUDE_LEAD, magnitudes)
                for_tile(step + MAGNITUDE_LEAD, fold)
                for_tile(step, lambda t: normalise(t, 0))
                for_tile(step + SUM_1_LEAD, sum_type_1)
                for_tile(step, lambda t: normalise(t, 1))
                for_tile(step, transpose)
                for_pair_starting_at(step + 1, clamp_sums)
                for_tile(step - 2, quantise)
                for_tile(step - 2, multiply)
                for_pair_starting_at(step + 1, invert_sums)
                for_tile(step - 1, lambda t: group(t, 0))
                for_tile(step - 1, lambda t: group(t, 1))
                for_tile(step + MAGNITUDE_LEAD, sum_fold)
                for_tile(step - STORE_LAG, store)
                for_graph_starting_at(step - 1, quantise_nodes)
                for_graph_starting_at(step, group_nodes)
